import numpy as np
import ml_dtypes

BF16 = ml_dtypes.bfloat16


def bf(x):
    return np.asarray(x, np.float32).astype(BF16)


def f32(x):
    return np.asarray(x, np.float32)


def f64(x):
    return np.asarray(x).astype(np.float64)


def striped(idx):
    return np.tile(idx.reshape(-1, 16).T, (8, 1))


D, S, N = 128, 512, 256
RATIO = 0.5


def setup_inputs():
    root = np.random.standard_normal((D, D))
    full = root @ root.T / D
    return {"wfc_t": bf(2.0 * np.random.standard_normal((D, S)) / np.sqrt(D)), "cov": bf(0.5 * (full + full.T)), "bfc": f32(0.1 * np.random.standard_normal((S, 1))), "offs": striped(np.random.permutation(np.tile(np.arange(S), 2))[:N])}


def reference(wfc_t, cov, bfc, offs):
    idx = offs[:16].T.reshape(-1)
    wt = f64(wfc_t)
    sw = f64(cov) @ wt
    q = np.sum(wt * sw, axis=0)[:, None]
    cross = sw.T @ wt[:, idx]
    return f64(bfc) + RATIO * 0.5 * (q - 2.0 * cross)

@@ -1,0 +1,60 @@
+import concourse.mybir as mybir
+
+FEATURES = 128
+CLASSES = 512
+SAMPLES = 256
+BLOCKS = CLASSES // 128
+
+FLOPS = 2 * FEATURES * FEATURES * CLASSES + 2 * FEATURES * CLASSES + 2 * FEATURES * CLASSES * SAMPLES
+
+BF16, F32, U16 = mybir.dt.bfloat16, mybir.dt.float32, mybir.dt.uint16
+MULT, ADD = mybir.AluOpType.mult, mybir.AluOpType.add
+IDENTITY = mybir.ActivationFunctionType.Identity
+
+
+def tile_predywiths_kernel(tc, wfc_t, cov, bfc, offs, out):
+    nc = tc.nc
+
+    bfc_by_block = bfc.rearrange("(b p) one -> p (b one)", p=128)
+    out_by_block = out.rearrange("(b p) j -> p b j", p=128)
+
+    with (
+        tc.tile_pool(name="held", bufs=1) as held,
+        tc.psum_pool(name="psum", bufs=1) as psum,
+    ):
+        table = held.tile([FEATURES, CLASSES], BF16, name="table")
+        nc.sync.dma_start(table[:], wfc_t)
+        offsets = held.tile([128, SAMPLES // 16], U16, name="offsets")
+        nc.sync.dma_start(offsets[:], offs)
+        cov_sb = held.tile([FEATURES, FEATURES], BF16, name="cov_sb")
+        nc.scalar.dma_start(cov_sb[:], cov)
+        bias = held.tile([128, BLOCKS], F32, name="bias")
+        with nc.allow_non_contiguous_dma(reason="bfc: one element to a partition"):
+            nc.scalar.dma_start(bias[:], bfc_by_block)
+        ones = held.tile([FEATURES, 1], BF16, name="ones")
+        nc.vector.memset(ones[:], 1.0)
+
+        sw_psum = psum.tile([FEATURES, CLASSES], F32, name="sw_psum")
+        nc.tensor.matmul(sw_psum[:], cov_sb[:], table[:], start=True, stop=True)
+        sw = held.tile([FEATURES, CLASSES], BF16, name="sw")
+        nc.vector.tensor_copy(sw[:], sw_psum[:])
+        products = held.tile([FEATURES, CLASSES], BF16, name="products")
+        nc.vector.tensor_tensor(products[:], table[:], sw[:], MULT)
+
+        q_psum = psum.tile([128, BLOCKS], F32, name="q_psum")
+        for b in range(BLOCKS):
+            nc.tensor.matmul(q_psum[:, b : b + 1], products[:, b * 128 : (b + 1) * 128], ones[:], start=True, stop=True)
+        shift = held.tile([128, BLOCKS], F32, name="shift")
+        nc.vector.scalar_tensor_tensor(shift[:], q_psum[:], 0.25, bias[:], MULT, ADD)
+
+        result = held.tile([128, BLOCKS, SAMPLES], F32, name="result")
+        for b in range(BLOCKS):
+            cross = psum.tile([128, SAMPLES], F32, name=f"cross{b}")
+            nc.tensor.matmul(
+                cross[:], sw[:, b * 128 : (b + 1) * 128], table[:].indirect(offsets[:]), start=True, stop=True
+            )
+            if b % 2 == 0:
+                nc.vector.tensor_scalar(result[:, b, :], cross[:], -0.5, shift[:, b : b + 1], MULT, ADD)
+            else:
+                nc.scalar.activation(result[:, b, :], cross[:], IDENTITY, bias=shift[:, b : b + 1], scale=-0.5)
+            nc.sync.dma_start(out_by_block[:, b, :], result[:, b, :])

@@ -15,8 +15,8 @@ IDENTITY = mybir.ActivationFunctionType.Identity
 def tile_predywiths_kernel(tc, wfc_t, cov, bfc, offs, out):
     nc = tc.nc
 
-    bfc_by_block = bfc.rearrange("(b p) one -> p (b one)", p=128)
-    out_by_block = out.rearrange("(b p) j -> p b j", p=128)
+    bfc_by_block = bfc.rearrange("(p b) one -> p (b one)", b=BLOCKS)
+    out_by_block = out.rearrange("(p b) j -> p b j", b=BLOCKS)
 
     with (
         tc.tile_pool(name="held", bufs=1) as held,
@@ -29,30 +29,29 @@ def tile_predywiths_kernel(tc, wfc_t, cov, bfc, offs, out):
         cov_sb = held.tile([FEATURES, FEATURES], BF16, name="cov_sb")
         nc.scalar.dma_start(cov_sb[:], cov)
         bias = held.tile([128, BLOCKS], F32, name="bias")
-        with nc.allow_non_contiguous_dma(reason="bfc: one element to a partition"):
-            nc.scalar.dma_start(bias[:], bfc_by_block)
+        nc.scalar.dma_start(bias[:], bfc_by_block)
         ones = held.tile([FEATURES, 1], BF16, name="ones")
         nc.vector.memset(ones[:], 1.0)
 
-        sw_psum = psum.tile([FEATURES, CLASSES], F32, name="sw_psum")
-        nc.tensor.matmul(sw_psum[:], cov_sb[:], table[:], start=True, stop=True)
-        sw = held.tile([FEATURES, CLASSES], BF16, name="sw")
+        table_by_block = table[:].rearrange("k (p b) -> k b p", b=BLOCKS)
+
+        sw_psum = psum.tile([FEATURES, BLOCKS, 128], F32, name="sw_psum")
+        nc.tensor.matmul(sw_psum[:], cov_sb[:], table_by_block, start=True, stop=True)
+        sw = held.tile([FEATURES, BLOCKS, 128], BF16, name="sw")
         nc.vector.tensor_copy(sw[:], sw_psum[:])
-        products = held.tile([FEATURES, CLASSES], BF16, name="products")
-        nc.vector.tensor_tensor(products[:], table[:], sw[:], MULT)
+        products = held.tile([FEATURES, BLOCKS, 128], BF16, name="products")
+        nc.vector.tensor_tensor(products[:], table_by_block, sw[:], MULT)
 
         q_psum = psum.tile([128, BLOCKS], F32, name="q_psum")
         for b in range(BLOCKS):
-            nc.tensor.matmul(q_psum[:, b : b + 1], products[:, b * 128 : (b + 1) * 128], ones[:], start=True, stop=True)
+            nc.tensor.matmul(q_psum[:, b : b + 1], products[:, b, :], ones[:], start=True, stop=True)
         shift = held.tile([128, BLOCKS], F32, name="shift")
         nc.vector.scalar_tensor_tensor(shift[:], q_psum[:], 0.25, bias[:], MULT, ADD)
 
         result = held.tile([128, BLOCKS, SAMPLES], F32, name="result")
         for b in range(BLOCKS):
             cross = psum.tile([128, SAMPLES], F32, name=f"cross{b}")
-            nc.tensor.matmul(
-                cross[:], sw[:, b * 128 : (b + 1) * 128], table[:].indirect(offsets[:]), start=True, stop=True
-            )
+            nc.tensor.matmul(cross[:], sw[:, b, :], table[:].indirect(offsets[:]), start=True, stop=True)
             if b % 2 == 0:
                 nc.vector.tensor_scalar(result[:, b, :], cross[:], -0.5, shift[:, b : b + 1], MULT, ADD)
             else:

@@ -15,8 +15,8 @@ IDENTITY = mybir.ActivationFunctionType.Identity
 def tile_predywiths_kernel(tc, wfc_t, cov, bfc, offs, out):
     nc = tc.nc
 
-    bfc_by_block = bfc.rearrange("(p b) one -> p (b one)", b=BLOCKS)
-    out_by_block = out.rearrange("(p b) j -> p b j", b=BLOCKS)
+    bfc_by_block = bfc.rearrange("(b p) one -> p (b one)", p=128)
+    out_by_block = out.rearrange("(b p) j -> p b j", p=128)
 
     with (
         tc.tile_pool(name="held", bufs=1) as held,
@@ -29,29 +29,32 @@ def tile_predywiths_kernel(tc, wfc_t, cov, bfc, offs, out):
         cov_sb = held.tile([FEATURES, FEATURES], BF16, name="cov_sb")
         nc.scalar.dma_start(cov_sb[:], cov)
         bias = held.tile([128, BLOCKS], F32, name="bias")
-        nc.scalar.dma_start(bias[:], bfc_by_block)
+        with nc.allow_non_contiguous_dma(reason="bfc: one element to a partition"):
+            nc.scalar.dma_start(bias[:], bfc_by_block)
         ones = held.tile([FEATURES, 1], BF16, name="ones")
         nc.vector.memset(ones[:], 1.0)
 
-        table_by_block = table[:].rearrange("k (p b) -> k b p", b=BLOCKS)
-
-        sw_psum = psum.tile([FEATURES, BLOCKS, 128], F32, name="sw_psum")
-        nc.tensor.matmul(sw_psum[:], cov_sb[:], table_by_block, start=True, stop=True)
-        sw = held.tile([FEATURES, BLOCKS, 128], BF16, name="sw")
-        nc.vector.tensor_copy(sw[:], sw_psum[:])
-        products = held.tile([FEATURES, BLOCKS, 128], BF16, name="products")
-        nc.vector.tensor_tensor(products[:], table_by_block, sw[:], MULT)
+        sw = held.tile([FEATURES, CLASSES], BF16, name="sw")
+        products = held.tile([FEATURES, CLASSES], BF16, name="products")
+        for b in range(BLOCKS):
+            block = slice(b * 128, (b + 1) * 128)
+            sw_psum = psum.tile([FEATURES, 128], BF16, name=f"sw_psum{b}", tag=f"bank{b}")
+            nc.tensor.matmul(sw_psum[:], cov_sb[:], table[:, block], start=True, stop=True)
+            nc.vector.tensor_tensor(products[:, block], table[:, block], sw_psum[:], MULT)
+            nc.scalar.copy(sw[:, block], sw_psum[:])
 
         q_psum = psum.tile([128, BLOCKS], F32, name="q_psum")
         for b in range(BLOCKS):
-            nc.tensor.matmul(q_psum[:, b : b + 1], products[:, b, :], ones[:], start=True, stop=True)
+            nc.tensor.matmul(q_psum[:, b : b + 1], products[:, b * 128 : (b + 1) * 128], ones[:], start=True, stop=True)
         shift = held.tile([128, BLOCKS], F32, name="shift")
         nc.vector.scalar_tensor_tensor(shift[:], q_psum[:], 0.25, bias[:], MULT, ADD)
 
         result = held.tile([128, BLOCKS, SAMPLES], F32, name="result")
         for b in range(BLOCKS):
-            cross = psum.tile([128, SAMPLES], F32, name=f"cross{b}")
-            nc.tensor.matmul(cross[:], sw[:, b, :], table[:].indirect(offsets[:]), start=True, stop=True)
+            cross = psum.tile([128, SAMPLES], F32, name=f"cross{b}", tag=f"bank{b}")
+            nc.tensor.matmul(
+                cross[:], sw[:, b * 128 : (b + 1) * 128], table[:].indirect(offsets[:]), start=True, stop=True
+            )
             if b % 2 == 0:
                 nc.vector.tensor_scalar(result[:, b, :], cross[:], -0.5, shift[:, b : b + 1], MULT, ADD)
             else:

@@ -4,6 +4,7 @@ FEATURES = 128
 CLASSES = 512
 SAMPLES = 256
 BLOCKS = CLASSES // 128
+WARM_UP_MATMULS = 4
 
 FLOPS = 2 * FEATURES * FEATURES * CLASSES + 2 * FEATURES * CLASSES + 2 * FEATURES * CLASSES * SAMPLES
 
@@ -33,6 +34,12 @@ def tile_predywiths_kernel(tc, wfc_t, cov, bfc, offs, out):
             nc.scalar.dma_start(bias[:], bfc_by_block)
         ones = held.tile([FEATURES, 1], BF16, name="ones")
         nc.vector.memset(ones[:], 1.0)
+
+        zeros = held.tile([128, CLASSES], BF16, name="zeros")
+        nc.vector.memset(zeros[:], 0.0)
+        warm_psum = psum.tile([128, CLASSES], F32, name="warm_psum")
+        for w in range(WARM_UP_MATMULS):
+            nc.tensor.matmul(warm_psum[:], zeros[:, 0:128], zeros[:], start=True, stop=True)
 
         sw = held.tile([FEATURES, CLASSES], BF16, name="sw")
         products = held.tile([FEATURES, CLASSES], BF16, name="products")

@@ -4,7 +4,7 @@ FEATURES = 128
 CLASSES = 512
 SAMPLES = 256
 BLOCKS = CLASSES // 128
-WARM_UP_MATMULS = 4
+CHUNK = 128
 
 FLOPS = 2 * FEATURES * FEATURES * CLASSES + 2 * FEATURES * CLASSES + 2 * FEATURES * CLASSES * SAMPLES
 
@@ -16,8 +16,8 @@ IDENTITY = mybir.ActivationFunctionType.Identity
 def tile_predywiths_kernel(tc, wfc_t, cov, bfc, offs, out):
     nc = tc.nc
 
-    bfc_by_block = bfc.rearrange("(b p) one -> p (b one)", p=128)
-    out_by_block = out.rearrange("(b p) j -> p b j", p=128)
+    bfc_by_block = bfc.rearrange("(p b) one -> p (b one)", b=BLOCKS)
+    out_by_block = out.rearrange("(p b) j -> p b j", b=BLOCKS)
 
     with (
         tc.tile_pool(name="held", bufs=1) as held,
@@ -30,38 +30,33 @@ def tile_predywiths_kernel(tc, wfc_t, cov, bfc, offs, out):
         cov_sb = held.tile([FEATURES, FEATURES], BF16, name="cov_sb")
         nc.scalar.dma_start(cov_sb[:], cov)
         bias = held.tile([128, BLOCKS], F32, name="bias")
-        with nc.allow_non_contiguous_dma(reason="bfc: one element to a partition"):
-            nc.scalar.dma_start(bias[:], bfc_by_block)
+        nc.scalar.dma_start(bias[:], bfc_by_block)
         ones = held.tile([FEATURES, 1], BF16, name="ones")
         nc.vector.memset(ones[:], 1.0)
 
-        zeros = held.tile([128, CLASSES], BF16, name="zeros")
-        nc.vector.memset(zeros[:], 0.0)
-        warm_psum = psum.tile([128, CLASSES], F32, name="warm_psum")
-        for w in range(WARM_UP_MATMULS):
-            nc.tensor.matmul(warm_psum[:], zeros[:, 0:128], zeros[:], start=True, stop=True)
-
-        sw = held.tile([FEATURES, CLASSES], BF16, name="sw")
+        sw = held.tile([FEATURES, BLOCKS, 128], BF16, name="sw")
         products = held.tile([FEATURES, CLASSES], BF16, name="products")
-        for b in range(BLOCKS):
-            block = slice(b * 128, (b + 1) * 128)
-            sw_psum = psum.tile([FEATURES, 128], BF16, name=f"sw_psum{b}", tag=f"bank{b}")
-            nc.tensor.matmul(sw_psum[:], cov_sb[:], table[:, block], start=True, stop=True)
-            nc.vector.tensor_tensor(products[:, block], table[:, block], sw_psum[:], MULT)
-            nc.scalar.copy(sw[:, block], sw_psum[:])
+        rows = CHUNK // BLOCKS
+        for c in range(CLASSES // CHUNK):
+            chunk = slice(c * CHUNK, (c + 1) * CHUNK)
+            sw_psum = psum.tile([FEATURES, CHUNK], BF16, name=f"sw_psum{c}", tag=f"bank{c}")
+            nc.tensor.matmul(sw_psum[:], cov_sb[:], table[:, chunk], start=True, stop=True)
+            nc.vector.tensor_tensor(products[:, chunk], table[:, chunk], sw_psum[:], MULT)
+            nc.scalar.copy(
+                sw[:, :, c * rows : (c + 1) * rows], sw_psum[:].rearrange("k (p b) -> k b p", b=BLOCKS)
+            )
 
+        products_by_block = products[:].rearrange("k (p b) -> k b p", b=BLOCKS)
         q_psum = psum.tile([128, BLOCKS], F32, name="q_psum")
         for b in range(BLOCKS):
-            nc.tensor.matmul(q_psum[:, b : b + 1], products[:, b * 128 : (b + 1) * 128], ones[:], start=True, stop=True)
+            nc.tensor.matmul(q_psum[:, b : b + 1], products_by_block[:, b, :], ones[:], start=True, stop=True)
         shift = held.tile([128, BLOCKS], F32, name="shift")
         nc.vector.scalar_tensor_tensor(shift[:], q_psum[:], 0.25, bias[:], MULT, ADD)
 
         result = held.tile([128, BLOCKS, SAMPLES], F32, name="result")
         for b in range(BLOCKS):
             cross = psum.tile([128, SAMPLES], F32, name=f"cross{b}", tag=f"bank{b}")
-            nc.tensor.matmul(
-                cross[:], sw[:, b * 128 : (b + 1) * 128], table[:].indirect(offsets[:]), start=True, stop=True
-            )
+            nc.tensor.matmul(cross[:], sw[:, b, :], table[:].indirect(offsets[:]), start=True, stop=True)
             if b % 2 == 0:
                 nc.vector.tensor_scalar(result[:, b, :], cross[:], -0.5, shift[:, b : b + 1], MULT, ADD)
             else:

@@ -4,7 +4,7 @@ FEATURES = 128
 CLASSES = 512
 SAMPLES = 256
 BLOCKS = CLASSES // 128
-CHUNK = 128
+WARM_UP_MATMULS, WARM_UP_COLUMNS = 6, 256
 
 FLOPS = 2 * FEATURES * FEATURES * CLASSES + 2 * FEATURES * CLASSES + 2 * FEATURES * CLASSES * SAMPLES
 
@@ -16,8 +16,8 @@ IDENTITY = mybir.ActivationFunctionType.Identity
 def tile_predywiths_kernel(tc, wfc_t, cov, bfc, offs, out):
     nc = tc.nc
 
-    bfc_by_block = bfc.rearrange("(p b) one -> p (b one)", b=BLOCKS)
-    out_by_block = out.rearrange("(p b) j -> p b j", b=BLOCKS)
+    bfc_by_block = bfc.rearrange("(b p) one -> p (b one)", p=128)
+    out_by_block = out.rearrange("(b p) j -> p b j", p=128)
 
     with (
         tc.tile_pool(name="held", bufs=1) as held,
@@ -30,33 +30,38 @@ def tile_predywiths_kernel(tc, wfc_t, cov, bfc, offs, out):
         cov_sb = held.tile([FEATURES, FEATURES], BF16, name="cov_sb")
         nc.scalar.dma_start(cov_sb[:], cov)
         bias = held.tile([128, BLOCKS], F32, name="bias")
-        nc.scalar.dma_start(bias[:], bfc_by_block)
+        with nc.allow_non_contiguous_dma(reason="bfc: one element to a partition"):
+            nc.scalar.dma_start(bias[:], bfc_by_block)
         ones = held.tile([FEATURES, 1], BF16, name="ones")
         nc.vector.memset(ones[:], 1.0)
 
-        sw = held.tile([FEATURES, BLOCKS, 128], BF16, name="sw")
-        products = held.tile([FEATURES, CLASSES], BF16, name="products")
-        rows = CHUNK // BLOCKS
-        for c in range(CLASSES // CHUNK):
-            chunk = slice(c * CHUNK, (c + 1) * CHUNK)
-            sw_psum = psum.tile([FEATURES, CHUNK], BF16, name=f"sw_psum{c}", tag=f"bank{c}")
-            nc.tensor.matmul(sw_psum[:], cov_sb[:], table[:, chunk], start=True, stop=True)
-            nc.vector.tensor_tensor(products[:, chunk], table[:, chunk], sw_psum[:], MULT)
-            nc.scalar.copy(
-                sw[:, :, c * rows : (c + 1) * rows], sw_psum[:].rearrange("k (p b) -> k b p", b=BLOCKS)
-            )
+        zeros = held.tile([128, WARM_UP_COLUMNS], BF16, name="zeros")
+        nc.gpsimd.memset(zeros[:], 0.0)
+        warm_psum = psum.tile([128, WARM_UP_COLUMNS], F32, name="warm_psum")
+        for w in range(WARM_UP_MATMULS):
+            nc.tensor.matmul(warm_psum[:], zeros[:, 0:128], zeros[:], start=True, stop=True)
 
-        products_by_block = products[:].rearrange("k (p b) -> k b p", b=BLOCKS)
+        sw = held.tile([FEATURES, CLASSES], BF16, name="sw")
+        products = held.tile([FEATURES, CLASSES], BF16, name="products")
+        for b in range(BLOCKS):
+            block = slice(b * 128, (b + 1) * 128)
+            sw_psum = psum.tile([FEATURES, 128], BF16, name=f"sw_psum{b}", tag=f"bank{b}")
+            nc.tensor.matmul(sw_psum[:], cov_sb[:], table[:, block], start=True, stop=True)
+            nc.vector.tensor_tensor(products[:, block], table[:, block], sw_psum[:], MULT)
+            nc.scalar.copy(sw[:, block], sw_psum[:])
+
         q_psum = psum.tile([128, BLOCKS], F32, name="q_psum")
         for b in range(BLOCKS):
-            nc.tensor.matmul(q_psum[:, b : b + 1], products_by_block[:, b, :], ones[:], start=True, stop=True)
+            nc.tensor.matmul(q_psum[:, b : b + 1], products[:, b * 128 : (b + 1) * 128], ones[:], start=True, stop=True)
         shift = held.tile([128, BLOCKS], F32, name="shift")
         nc.vector.scalar_tensor_tensor(shift[:], q_psum[:], 0.25, bias[:], MULT, ADD)
 
         result = held.tile([128, BLOCKS, SAMPLES], F32, name="result")
         for b in range(BLOCKS):
             cross = psum.tile([128, SAMPLES], F32, name=f"cross{b}", tag=f"bank{b}")
-            nc.tensor.matmul(cross[:], sw[:, b, :], table[:].indirect(offsets[:]), start=True, stop=True)
+            nc.tensor.matmul(
+                cross[:], sw[:, b * 128 : (b + 1) * 128], table[:].indirect(offsets[:]), start=True, stop=True
+            )
             if b % 2 == 0:
                 nc.vector.tensor_scalar(result[:, b, :], cross[:], -0.5, shift[:, b : b + 1], MULT, ADD)
             else:

@@ -23,15 +23,15 @@ def tile_predywiths_kernel(tc, wfc_t, cov, bfc, offs, out):
         tc.tile_pool(name="held", bufs=1) as held,
         tc.psum_pool(name="psum", bufs=1) as psum,
     ):
+        cov_sb = held.tile([FEATURES, FEATURES], BF16, name="cov_sb")
+        nc.sync.dma_start(cov_sb[:], cov)
         table = held.tile([FEATURES, CLASSES], BF16, name="table")
         nc.sync.dma_start(table[:], wfc_t)
         offsets = held.tile([128, SAMPLES // 16], U16, name="offsets")
         nc.sync.dma_start(offsets[:], offs)
-        cov_sb = held.tile([FEATURES, FEATURES], BF16, name="cov_sb")
-        nc.scalar.dma_start(cov_sb[:], cov)
         bias = held.tile([128, BLOCKS], F32, name="bias")
         with nc.allow_non_contiguous_dma(reason="bfc: one element to a partition"):
-            nc.scalar.dma_start(bias[:], bfc_by_block)
+            nc.sync.dma_start(bias[:], bfc_by_block)
         ones = held.tile([FEATURES, 1], BF16, name="ones")
         nc.vector.memset(ones[:], 1.0)
 

@@ -4,7 +4,7 @@ FEATURES = 128
 CLASSES = 512
 SAMPLES = 256
 BLOCKS = CLASSES // 128
-WARM_UP_MATMULS, WARM_UP_COLUMNS = 6, 256
+WARM_UP_MATMULS, WARM_UP_COLUMNS = 7, 256
 
 FLOPS = 2 * FEATURES * FEATURES * CLASSES + 2 * FEATURES * CLASSES + 2 * FEATURES * CLASSES * SAMPLES
 
@@ -35,11 +35,15 @@ def tile_predywiths_kernel(tc, wfc_t, cov, bfc, offs, out):
         ones = held.tile([FEATURES, 1], BF16, name="ones")
         nc.vector.memset(ones[:], 1.0)
 
-        zeros = held.tile([128, WARM_UP_COLUMNS], BF16, name="zeros")
-        nc.gpsimd.memset(zeros[:], 0.0)
         warm_psum = psum.tile([128, WARM_UP_COLUMNS], F32, name="warm_psum")
         for w in range(WARM_UP_MATMULS):
-            nc.tensor.matmul(warm_psum[:], zeros[:, 0:128], zeros[:], start=True, stop=True)
+            nc.tensor.matmul(
+                warm_psum[:],
+                ones[:].to_broadcast([FEATURES, 128]),
+                ones[:].to_broadcast([FEATURES, WARM_UP_COLUMNS]),
+                start=True,
+                stop=True,
+            )
 
         sw = held.tile([FEATURES, CLASSES], BF16, name="sw")
         products = held.tile([FEATURES, CLASSES], BF16, name="products")

import concourse.mybir as mybir

FEATURES = 128
CLASSES = 512
SAMPLES = 256
BLOCKS = CLASSES // 128
WARM_UP_MATMULS, WARM_UP_COLUMNS = 7, 256

FLOPS = 2 * FEATURES * FEATURES * CLASSES + 2 * FEATURES * CLASSES + 2 * FEATURES * CLASSES * SAMPLES

BF16, F32, U16 = mybir.dt.bfloat16, mybir.dt.float32, mybir.dt.uint16
MULT, ADD = mybir.AluOpType.mult, mybir.AluOpType.add
IDENTITY = mybir.ActivationFunctionType.Identity


def tile_predywiths_kernel(tc, wfc_t, cov, bfc, offs, out):
    nc = tc.nc

    bfc_by_block = bfc.rearrange("(b p) one -> p (b one)", p=128)
    out_by_block = out.rearrange("(b p) j -> p b j", p=128)

    with (
        tc.tile_pool(name="held", bufs=1) as held,
        tc.psum_pool(name="psum", bufs=1) as psum,
    ):
        cov_sb = held.tile([FEATURES, FEATURES], BF16, name="cov_sb")
        nc.sync.dma_start(cov_sb[:], cov)
        table = held.tile([FEATURES, CLASSES], BF16, name="table")
        nc.sync.dma_start(table[:], wfc_t)
        offsets = held.tile([128, SAMPLES // 16], U16, name="offsets")
        nc.sync.dma_start(offsets[:], offs)
        bias = held.tile([128, BLOCKS], F32, name="bias")
        with nc.allow_non_contiguous_dma(reason="bfc: one element to a partition"):
            nc.sync.dma_start(bias[:], bfc_by_block)
        ones = held.tile([FEATURES, 1], BF16, name="ones")
        nc.vector.memset(ones[:], 1.0)

        warm_psum = psum.tile([128, WARM_UP_COLUMNS], F32, name="warm_psum")
        for w in range(WARM_UP_MATMULS):
            nc.tensor.matmul(
                warm_psum[:],
                ones[:].to_broadcast([FEATURES, 128]),
                ones[:].to_broadcast([FEATURES, WARM_UP_COLUMNS]),
                start=True,
                stop=True,
            )

        sw = held.tile([FEATURES, CLASSES], BF16, name="sw")
        products = held.tile([FEATURES, CLASSES], BF16, name="products")
        for b in range(BLOCKS):
            block = slice(b * 128, (b + 1) * 128)
            sw_psum = psum.tile([FEATURES, 128], BF16, name=f"sw_psum{b}", tag=f"bank{b}")
            nc.tensor.matmul(sw_psum[:], cov_sb[:], table[:, block], start=True, stop=True)
            nc.vector.tensor_tensor(products[:, block], table[:, block], sw_psum[:], MULT)
            nc.scalar.copy(sw[:, block], sw_psum[:])

        q_psum = psum.tile([128, BLOCKS], F32, name="q_psum")
        for b in range(BLOCKS):
            nc.tensor.matmul(q_psum[:, b : b + 1], products[:, b * 128 : (b + 1) * 128], ones[:], start=True, stop=True)
        shift = held.tile([128, BLOCKS], F32, name="shift")
        nc.vector.scalar_tensor_tensor(shift[:], q_psum[:], 0.25, bias[:], MULT, ADD)

        result = held.tile([128, BLOCKS, SAMPLES], F32, name="result")
        for b in range(BLOCKS):
            cross = psum.tile([128, SAMPLES], F32, name=f"cross{b}", tag=f"bank{b}")
            nc.tensor.matmul(
                cross[:], sw[:, b * 128 : (b + 1) * 128], table[:].indirect(offsets[:]), start=True, stop=True
            )
            if b % 2 == 0:
                nc.vector.tensor_scalar(result[:, b, :], cross[:], -0.5, shift[:, b : b + 1], MULT, ADD)
            else:
                nc.scalar.activation(result[:, b, :], cross[:], IDENTITY, bias=shift[:, b : b + 1], scale=-0.5)
            nc.sync.dma_start(out_by_block[:, b, :], result[:, b, :])
